import numpy as np
import ml_dtypes


def mxq(x, axis, fmt="e4m3"):
    dtype, down = {"e4m3": (ml_dtypes.float8_e4m3fn, 7), "e5m2": (ml_dtypes.float8_e5m2, 14)}[fmt]
    v = np.moveaxis(np.asarray(x, np.float32).astype(ml_dtypes.bfloat16).astype(np.float64), axis, -1)
    blocks = v.reshape(v.shape[:-1] + (-1, 32))
    amax = np.abs(blocks).max(-1, keepdims=True)
    byte = np.maximum(np.where(amax > 0, np.frexp(amax)[1] - 1 + 127, 0) - down, 1)
    scale = np.exp2(byte - 127.0)
    codes = (blocks / scale).astype(np.float32).astype(dtype).astype(np.float64)
    return np.moveaxis((codes * scale).reshape(v.shape), -1, axis)


WIDE = False


def mx_kscale(k):
    if not WIDE:
        return np.ones(k)
    levels = np.array([10, -10, 5, -5, 0])
    a = np.random.permutation(np.resize(levels, k // 512 * 4)).reshape(k // 512, 4)
    idx = np.arange(k)
    return np.exp2(a[idx // 512, idx % 128 // 32])


BF16 = ml_dtypes.bfloat16


def bf(x):
    return np.asarray(x, np.float32).astype(BF16)


def f64(x):
    return np.asarray(x).astype(np.float64)


E2M1 = np.array([0.0, 0.5, 1.0, 1.5, 2.0, 3.0, 4.0, 6.0, -0.0, -0.5, -1.0, -1.5, -2.0, -3.0, -4.0, -6.0])


def pack_weight(w, fmt):
    k, n = w.shape
    w = f64(bf(w)).reshape(k // 32, 32, n)
    amax = np.abs(w).max(1)
    if fmt == "e4m3":
        byte = np.frexp(amax)[1] - 1 + 127 - 7
    else:
        mant, ex = np.frexp(amax / 6.0)
        byte = np.where(mant > 0.5, ex, ex - 1) + 127
    byte = np.clip(np.where(amax > 0, byte, 1), 1, 254)
    scaled = (w * np.exp2(127.0 - byte)[:, None, :]).reshape(k, n).astype(np.float32)
    by_word = np.ascontiguousarray(scaled.reshape(k // 512, 128, 4, n).transpose(0, 1, 3, 2))
    if fmt == "e4m3":
        words = by_word.astype(ml_dtypes.float8_e4m3fn).view(np.uint8)
    else:
        c = by_word.astype(ml_dtypes.float4_e2m1fn).view(np.uint8) & 0xF
        words = c[..., 0::2] | (c[..., 1::2] << 4)
    return np.ascontiguousarray(words), np.ascontiguousarray(byte.astype(np.uint8).reshape(k // 512, 16, n))


def unpack_weight(words, scales, fmt):
    g, p, n, _ = words.shape
    if fmt == "e4m3":
        vals = np.ascontiguousarray(words).view(ml_dtypes.float8_e4m3fn).astype(np.float64)
    else:
        nib = np.empty((g, p, n, 4), np.uint8)
        nib[..., 0::2] = words & 0xF
        nib[..., 1::2] = words >> 4
        vals = E2M1[nib]
    vals = vals * np.repeat(np.exp2(scales.astype(np.float64) - 127.0), 8, axis=1)[..., None]
    return vals.transpose(0, 1, 3, 2).reshape(g * 512, n)


B, L, C, K = 128, 8, 512, 5
F = C
BN_EPS = 1e-3
LEAKY_ALPHA = 0.3


def leaky(v):
    return np.where(v >= 0, v, LEAKY_ALPHA * v)


def bn(v, gamma, beta, mean, var):
    return gamma * (v - mean) * (1.0 / np.sqrt(var + BN_EPS)) + beta


def setup_inputs():
    s = mx_kscale(C)
    x = bf(np.random.standard_normal((B, L, C)) * s)
    k1 = np.random.standard_normal((K, L, C, F)) * 0.14 / np.sqrt(K * C) / s[:, None]
    k1_words, k1_scales = pack_weight(k1.reshape(-1, F), "e4m3")
    return {"x": x,
            "k1_words": k1_words,
            "k1_scales": k1_scales,
            "b1": bf(np.random.standard_normal((L, F)) * 0.03),
            "gamma1": bf(1.0 + 0.1 * np.random.standard_normal(F)),
            "beta1": bf(np.random.standard_normal(F) * 0.2),
            "mean1": bf(np.random.standard_normal(F) * 0.05),
            "var1": bf(np.random.uniform(0.01, 0.03, F))}


def reference(x, k1_words, k1_scales, b1, gamma1, beta1, mean1, var1):
    xq = mxq(f64(x).transpose(1, 0, 2), 2, "e4m3")
    k = unpack_weight(k1_words, k1_scales, "e4m3").reshape(K, L, C, F)
    out = 2.0 * f64(b1)
    for i in range(k.shape[0]):
        step = (i // 2) * (-1 if i % 2 == 1 else 1)
        ki = k[i][(np.arange(L) + step) % L] if step != 0 else k[i]
        p = xq @ ki
        p = np.roll(p, step, axis=0) if step != 0 else p
        out = out + p.transpose(1, 0, 2)
    return leaky(bn(out, f64(gamma1), f64(beta1), f64(mean1), f64(var1)))

@@ -1,0 +1,206 @@
+from contextlib import ExitStack
+
+import concourse.mybir as mybir
+from concourse.masks import make_identity
+
+F32 = mybir.dt.float32
+BF16 = mybir.dt.bfloat16
+I32 = mybir.dt.int32
+U8 = mybir.dt.uint8
+FP8X4 = mybir.dt.float8_e4m3fn_x4
+ALU = mybir.AluOpType
+
+P = 128
+POSITIONS = 8
+CHANNELS = 512
+FILTERS = 512
+TAPS = 5
+STEP = (0, 0, 1, -1, 2)
+BN_EPS = 1e-3
+LEAKY_ALPHA = 0.3
+CHUNKS = FILTERS // P
+
+PLANES_PER_SLOT = 4
+SLOTS = TAPS * POSITIONS // PLANES_PER_SLOT
+QUADRANTS = 4
+SCALE_LEAD = 4
+
+FLOPS = 2 * P * POSITIONS * TAPS * CHANNELS * FILTERS
+
+
+def plane_place(tap, position):
+    if tap < PLANES_PER_SLOT:
+        return position, 4 * tap
+    return POSITIONS + position // PLANES_PER_SLOT, 4 * (position % PLANES_PER_SLOT)
+
+
+def tile_residualblock5_pa_e_kernel(
+    tc, x, k1_words, k1_scales, b1, gamma1, beta1, mean1, var1, out
+):
+    nc = tc.nc
+    with ExitStack() as ctx:
+        ctx.enter_context(tc.manual_schedule())
+        keep = ctx.enter_context(tc.tile_pool(name="keep", bufs=1))
+        work = ctx.enter_context(tc.tile_pool(name="work", bufs=4))
+        setup_psum = ctx.enter_context(tc.psum_pool(name="setup_psum", bufs=4))
+        acc_psum = ctx.enter_context(tc.psum_pool(name="acc_psum", bufs=4))
+
+        x_sb = keep.tile([P, POSITIONS * CHANNELS], BF16)
+        grouped = keep.tile([P, POSITIONS * CHANNELS], BF16, align_bytes=64)
+        x_codes = keep.tile([P, POSITIONS * P], I32, align_bytes=64)
+        x_scales = keep.tile([P, POSITIONS * P], U8, align_bytes=64)
+        planes = keep.tile([P, SLOTS * FILTERS], U8, align_bytes=64)
+        weights = {}
+        for position in range(POSITIONS):
+            for tap in range(TAPS):
+                weights[(tap, position)] = keep.tile(
+                    [P, FILTERS], I32, align_bytes=64, name="w%d_%d" % (tap, position)
+                )
+        vec_rows = keep.tile([P, P], BF16)
+        ident_f32 = keep.tile([P, P], F32)
+        ident_bf16 = keep.tile([P, P], BF16)
+
+        nc.vector.memset(planes[:].bitcast(I32), 0)
+        nc.vector.memset(vec_rows[:], 0.0)
+
+        nc.gpsimd.dma_start(
+            out=vec_rows[0 : POSITIONS * CHUNKS, :],
+            in_=b1.rearrange("l (c n) -> (l c) n", n=P),
+        )
+        for v, vector in enumerate((gamma1, beta1, mean1, var1)):
+            row = (POSITIONS + v) * CHUNKS
+            nc.gpsimd.dma_start(
+                out=vec_rows[row : row + CHUNKS, :],
+                in_=vector.rearrange("(c n) -> c n", n=P),
+            )
+        make_identity(nc, ident_f32[:])
+
+        nc.sync.dma_start(out=x_sb[:], in_=x.rearrange("b l c -> b (l c)"))
+
+        scales_by_position = k1_scales.rearrange("(i l) q n -> l i q n", l=POSITIONS)
+
+        def load_scales(slot, quadrant):
+            rows = slice(4 * quadrant, 4 * quadrant + 4)
+            if slot < POSITIONS:
+                source = scales_by_position[slot, 0:PLANES_PER_SLOT, rows, :]
+            else:
+                first = PLANES_PER_SLOT * POSITIONS + PLANES_PER_SLOT * (slot - POSITIONS)
+                source = k1_scales[first : first + PLANES_PER_SLOT, rows, :]
+            nc.sync.dma_start(
+                out=planes[
+                    32 * quadrant : 32 * quadrant + 16, FILTERS * slot : FILTERS * (slot + 1)
+                ].bitcast(I32),
+                in_=source.bitcast(I32),
+            )
+
+        def load_weight(tap, position):
+            nc.sync.dma_start(
+                out=weights[(tap, position)][:],
+                in_=k1_words[POSITIONS * tap + position].rearrange("p n t -> p (n t)").bitcast(I32),
+            )
+
+        scale_loads = []
+        for half in range(2):
+            for slot in [POSITIONS + half] + list(range(4 * half, 4 * half + 4)):
+                for quadrant in range(QUADRANTS):
+                    scale_loads.append((slot, quadrant))
+        weight_loads = [(tap, position) for position in range(POSITIONS) for tap in range(TAPS)]
+
+        for slot, quadrant in scale_loads[:SCALE_LEAD]:
+            load_scales(slot, quadrant)
+        for n, (tap, position) in enumerate(weight_loads):
+            load_weight(tap, position)
+            if SCALE_LEAD + n < len(scale_loads):
+                slot, quadrant = scale_loads[SCALE_LEAD + n]
+                load_scales(slot, quadrant)
+
+        nc.vector.tensor_copy(out=ident_bf16[:], in_=ident_f32[:])
+
+        x_words = x_sb[:].bitcast(F32)
+        grouped_words = grouped[:].bitcast(F32)
+        WORDS = CHANNELS // 2
+        for pair in range(POSITIONS // 2):
+            xt = setup_psum.tile([P, 2, 2, P], F32, tag="setup", name="xt")
+            for a in range(2):
+                first = WORDS * (2 * pair + a)
+                for u in range(2):
+                    nc.tensor.transpose(
+                        xt[:, a, u, :], x_words[:, first + u : first + WORDS : 2], ident_f32[:]
+                    )
+            dest = grouped_words[:, 2 * WORDS * pair : 2 * WORDS * (pair + 1)].rearrange(
+                "p (a b u) -> p a b u", a=2, u=2
+            )
+            source = xt[:].rearrange("p a u b -> p a b u")
+            if pair % 2 == 0:
+                nc.vector.tensor_copy(out=dest, in_=source)
+            else:
+                nc.scalar.copy(out=dest, in_=source)
+        for pair in range(POSITIONS // 2):
+            nc.vector.quantize_mx(
+                out=x_codes[:, 2 * P * pair : 2 * P * (pair + 1)].bitcast(FP8X4),
+                scales=x_scales[:, 2 * P * pair : 2 * P * (pair + 1)],
+                in_=grouped[:, 2 * CHANNELS * pair : 2 * CHANNELS * (pair + 1)],
+            )
+
+        rows_t = setup_psum.tile([P, P], BF16, tag="setup", name="rows_t")
+        nc.tensor.transpose(rows_t[:], vec_rows[:], ident_bf16[:])
+        N_COLS = (POSITIONS + 4) * CHUNKS
+        cols = keep.tile([P, N_COLS], F32)
+        nc.vector.tensor_copy(out=cols[:], in_=rows_t[:, 0:N_COLS])
+        b1_c = cols[:, 0 : POSITIONS * CHUNKS].rearrange("p (l c) -> p l c", c=CHUNKS)
+
+        def vec_col(v):
+            return cols[:, (POSITIONS + v) * CHUNKS : (POSITIONS + v + 1) * CHUNKS]
+
+        def over_positions(ap):
+            return ap.unsqueeze(1).to_broadcast([P, POSITIONS, CHUNKS])
+
+        gamma_c, beta_c, mean_c, var_c = vec_col(0), vec_col(1), vec_col(2), vec_col(3)
+        folded = keep.tile([P, (POSITIONS + 1) * CHUNKS], F32)
+        shift_c = folded[:, 0 : POSITIONS * CHUNKS].rearrange("p (l c) -> p l c", c=CHUNKS)
+        gain_c = folded[:, POSITIONS * CHUNKS : (POSITIONS + 1) * CHUNKS]
+        std_c = keep.tile([P, CHUNKS], F32)
+        nc.vector.tensor_scalar_add(out=std_c[:], in0=var_c, scalar1=BN_EPS)
+        nc.scalar.sqrt(out=std_c[:], in_=std_c[:])
+        nc.vector.reciprocal(out=std_c[:], in_=std_c[:])
+        nc.vector.tensor_tensor(out=gain_c, in0=gamma_c, in1=std_c[:], op=ALU.mult)
+        nc.vector.scalar_tensor_tensor(
+            out=shift_c, in0=b1_c, scalar=2.0, in1=over_positions(mean_c),
+            op0=ALU.mult, op1=ALU.subtract,
+        )
+        nc.vector.tensor_tensor(out=shift_c, in0=shift_c, in1=over_positions(gain_c), op=ALU.mult)
+        nc.vector.tensor_tensor(out=shift_c, in0=shift_c, in1=over_positions(beta_c), op=ALU.add)
+
+        spread = keep.tile([P, POSITIONS + 1, FILTERS], F32)
+        for v in range(POSITIONS + 1):
+            spread_ps = setup_psum.tile([P, FILTERS], F32, tag="setup", name="spread_ps")
+            for c in range(CHUNKS):
+                col = CHUNKS * v + c
+                nc.tensor.transpose(
+                    spread_ps[:, P * c : P * (c + 1)],
+                    folded[:, col : col + 1].to_broadcast([P, P]),
+                    ident_f32[:],
+                )
+            nc.scalar.copy(out=spread[:, v, :], in_=spread_ps[:])
+
+        for position in range(POSITIONS):
+            acc = acc_psum.tile([P, FILTERS], F32)
+            for tap in range(TAPS):
+                x_pos = (position - STEP[tap]) % POSITIONS
+                slot, offset = plane_place(tap, position)
+                nc.tensor.matmul_mx(
+                    out=acc[:],
+                    lhsT=x_codes[:, P * x_pos : P * (x_pos + 1)].bitcast(FP8X4),
+                    lhsT_scale=x_scales[:, P * x_pos : P * (x_pos + 1)],
+                    rhs=weights[(tap, position)][:].bitcast(FP8X4),
+                    rhs_scale=planes[offset:P, FILTERS * slot : FILTERS * (slot + 1)],
+                    start=(tap == 0),
+                    stop=(tap == TAPS - 1),
+                )
+            z = work.tile([P, FILTERS], F32)
+            nc.vector.tensor_tensor(out=z[:], in0=acc[:], in1=spread[:, POSITIONS, :], op=ALU.mult)
+            nc.vector.tensor_tensor(out=z[:], in0=z[:], in1=spread[:, position, :], op=ALU.add)
+            nc.vector.scalar_tensor_tensor(
+                out=z[:], in0=z[:], scalar=LEAKY_ALPHA, in1=z[:], op0=ALU.mult, op1=ALU.max
+            )
+            nc.scalar.dma_start(out=out[:, position, :], in_=z[:])

@@ -23,15 +23,13 @@ CHUNKS = FILTERS // P
 PLANES_PER_SLOT = 4
 SLOTS = TAPS * POSITIONS // PLANES_PER_SLOT
 QUADRANTS = 4
-SCALE_LEAD = 4
 
 FLOPS = 2 * P * POSITIONS * TAPS * CHANNELS * FILTERS
 
 
 def plane_place(tap, position):
-    if tap < PLANES_PER_SLOT:
-        return position, 4 * tap
-    return POSITIONS + position // PLANES_PER_SLOT, 4 * (position % PLANES_PER_SLOT)
+    matrix = POSITIONS * tap + position
+    return matrix % SLOTS, 4 * (matrix // SLOTS)
 
 
 def tile_residualblock5_pa_e_kernel(
@@ -41,7 +39,7 @@ def tile_residualblock5_pa_e_kernel(
     with ExitStack() as ctx:
         ctx.enter_context(tc.manual_schedule())
         keep = ctx.enter_context(tc.tile_pool(name="keep", bufs=1))
-        work = ctx.enter_context(tc.tile_pool(name="work", bufs=4))
+        work = ctx.enter_context(tc.tile_pool(name="work", bufs=POSITIONS))
         setup_psum = ctx.enter_context(tc.psum_pool(name="setup_psum", bufs=4))
         acc_psum = ctx.enter_context(tc.psum_pool(name="acc_psum", bufs=4))
 
@@ -50,71 +48,78 @@ def tile_residualblock5_pa_e_kernel(
         x_codes = keep.tile([P, POSITIONS * P], I32, align_bytes=64)
         x_scales = keep.tile([P, POSITIONS * P], U8, align_bytes=64)
         planes = keep.tile([P, SLOTS * FILTERS], U8, align_bytes=64)
-        weights = {}
-        for position in range(POSITIONS):
-            for tap in range(TAPS):
-                weights[(tap, position)] = keep.tile(
-                    [P, FILTERS], I32, align_bytes=64, name="w%d_%d" % (tap, position)
-                )
+        weights = [
+            keep.tile([P, TAPS, FILTERS], I32, align_bytes=64, name="w%d" % position)
+            for position in range(POSITIONS)
+        ]
         vec_rows = keep.tile([P, P], BF16)
         ident_f32 = keep.tile([P, P], F32)
         ident_bf16 = keep.tile([P, P], BF16)
 
-        nc.vector.memset(planes[:].bitcast(I32), 0)
+        make_identity(nc, ident_f32[:])
         nc.vector.memset(vec_rows[:], 0.0)
+        nc.vector.memset(planes[:].bitcast(I32), 0)
 
-        nc.gpsimd.dma_start(
+        nc.scalar.dma_start(
             out=vec_rows[0 : POSITIONS * CHUNKS, :],
             in_=b1.rearrange("l (c n) -> (l c) n", n=P),
         )
         for v, vector in enumerate((gamma1, beta1, mean1, var1)):
             row = (POSITIONS + v) * CHUNKS
-            nc.gpsimd.dma_start(
+            nc.scalar.dma_start(
                 out=vec_rows[row : row + CHUNKS, :],
                 in_=vector.rearrange("(c n) -> c n", n=P),
             )
-        make_identity(nc, ident_f32[:])
 
         nc.sync.dma_start(out=x_sb[:], in_=x.rearrange("b l c -> b (l c)"))
 
-        scales_by_position = k1_scales.rearrange("(i l) q n -> l i q n", l=POSITIONS)
+        scale_rows = k1_scales.rearrange(
+            "(j s) (q r) n -> q r j s n", j=PLANES_PER_SLOT, r=4
+        )
+        for r in range(4):
+            for quadrant in range(QUADRANTS):
+                first = 32 * quadrant + r
+                nc.sync.dma_start(
+                    out=planes[first : first + 16 : 4, :].bitcast(I32),
+                    in_=scale_rows[quadrant, r].bitcast(I32),
+                )
 
-        def load_scales(slot, quadrant):
-            rows = slice(4 * quadrant, 4 * quadrant + 4)
-            if slot < POSITIONS:
-                source = scales_by_position[slot, 0:PLANES_PER_SLOT, rows, :]
-            else:
-                first = PLANES_PER_SLOT * POSITIONS + PLANES_PER_SLOT * (slot - POSITIONS)
-                source = k1_scales[first : first + PLANES_PER_SLOT, rows, :]
+        words_by_position = k1_words.rearrange("(i l) p n t -> l p i (n t)", l=POSITIONS)
+        for position in range(POSITIONS):
             nc.sync.dma_start(
-                out=planes[
-                    32 * quadrant : 32 * quadrant + 16, FILTERS * slot : FILTERS * (slot + 1)
-                ].bitcast(I32),
-                in_=source.bitcast(I32),
+                out=weights[position][:], in_=words_by_position[position].bitcast(I32)
             )
-
-        def load_weight(tap, position):
-            nc.sync.dma_start(
-                out=weights[(tap, position)][:],
-                in_=k1_words[POSITIONS * tap + position].rearrange("p n t -> p (n t)").bitcast(I32),
-            )
-
-        scale_loads = []
-        for half in range(2):
-            for slot in [POSITIONS + half] + list(range(4 * half, 4 * half + 4)):
-                for quadrant in range(QUADRANTS):
-                    scale_loads.append((slot, quadrant))
-        weight_loads = [(tap, position) for position in range(POSITIONS) for tap in range(TAPS)]
-
-        for slot, quadrant in scale_loads[:SCALE_LEAD]:
-            load_scales(slot, quadrant)
-        for n, (tap, position) in enumerate(weight_loads):
-            load_weight(tap, position)
-            if SCALE_LEAD + n < len(scale_loads):
-                slot, quadrant = scale_loads[SCALE_LEAD + n]
-                load_scales(slot, quadrant)
 
         nc.vector.tensor_copy(out=ident_bf16[:], in_=ident_f32[:])
+
+        rows_t = setup_psum.tile([P, P], BF16, tag="setup", name="rows_t")
+        nc.tensor.transpose(rows_t[:], vec_rows[:], ident_bf16[:])
+        N_COLS = (POSITIONS + 4) * CHUNKS
+        cols = keep.tile([P, N_COLS], F32)
+        nc.vector.tensor_copy(out=cols[:], in_=rows_t[:, 0:N_COLS])
+        b1_c = cols[:, 0 : POSITIONS * CHUNKS].rearrange("p (l c) -> p l c", c=CHUNKS)
+
+        def vec_col(v):
+            return cols[:, (POSITIONS + v) * CHUNKS : (POSITIONS + v + 1) * CHUNKS]
+
+        def over_positions(ap):
+            return ap.unsqueeze(1).to_broadcast([P, POSITIONS, CHUNKS])
+
+        gamma_c, beta_c, mean_c, var_c = vec_col(0), vec_col(1), vec_col(2), vec_col(3)
+        folded = keep.tile([P, (1 + POSITIONS) * CHUNKS], F32)
+        gain_c = folded[:, 0:CHUNKS]
+        shift_c = folded[:, CHUNKS : (1 + POSITIONS) * CHUNKS].rearrange("p (l c) -> p l c", c=CHUNKS)
+        std_c = keep.tile([P, CHUNKS], F32)
+        nc.vector.tensor_scalar_add(out=std_c[:], in0=var_c, scalar1=BN_EPS)
+        nc.scalar.sqrt(out=std_c[:], in_=std_c[:])
+        nc.vector.reciprocal(out=std_c[:], in_=std_c[:])
+        nc.vector.tensor_tensor(out=gain_c, in0=gamma_c, in1=std_c[:], op=ALU.mult)
+        nc.vector.scalar_tensor_tensor(
+            out=shift_c, in0=b1_c, scalar=2.0, in1=over_positions(mean_c),
+            op0=ALU.mult, op1=ALU.subtract,
+        )
+        nc.vector.tensor_tensor(out=shift_c, in0=shift_c, in1=over_positions(gain_c), op=ALU.mult)
+        nc.vector.tensor_tensor(out=shift_c, in0=shift_c, in1=over_positions(beta_c), op=ALU.add)
 
         x_words = x_sb[:].bitcast(F32)
         grouped_words = grouped[:].bitcast(F32)
@@ -142,37 +147,8 @@ def tile_residualblock5_pa_e_kernel(
                 in_=grouped[:, 2 * CHANNELS * pair : 2 * CHANNELS * (pair + 1)],
             )
 
-        rows_t = setup_psum.tile([P, P], BF16, tag="setup", name="rows_t")
-        nc.tensor.transpose(rows_t[:], vec_rows[:], ident_bf16[:])
-        N_COLS = (POSITIONS + 4) * CHUNKS
-        cols = keep.tile([P, N_COLS], F32)
-        nc.vector.tensor_copy(out=cols[:], in_=rows_t[:, 0:N_COLS])
-        b1_c = cols[:, 0 : POSITIONS * CHUNKS].rearrange("p (l c) -> p l c", c=CHUNKS)
-
-        def vec_col(v):
-            return cols[:, (POSITIONS + v) * CHUNKS : (POSITIONS + v + 1) * CHUNKS]
-
-        def over_positions(ap):
-            return ap.unsqueeze(1).to_broadcast([P, POSITIONS, CHUNKS])
-
-        gamma_c, beta_c, mean_c, var_c = vec_col(0), vec_col(1), vec_col(2), vec_col(3)
-        folded = keep.tile([P, (POSITIONS + 1) * CHUNKS], F32)
-        shift_c = folded[:, 0 : POSITIONS * CHUNKS].rearrange("p (l c) -> p l c", c=CHUNKS)
-        gain_c = folded[:, POSITIONS * CHUNKS : (POSITIONS + 1) * CHUNKS]
-        std_c = keep.tile([P, CHUNKS], F32)
-        nc.vector.tensor_scalar_add(out=std_c[:], in0=var_c, scalar1=BN_EPS)
-        nc.scalar.sqrt(out=std_c[:], in_=std_c[:])
-        nc.vector.reciprocal(out=std_c[:], in_=std_c[:])
-        nc.vector.tensor_tensor(out=gain_c, in0=gamma_c, in1=std_c[:], op=ALU.mult)
-        nc.vector.scalar_tensor_tensor(
-            out=shift_c, in0=b1_c, scalar=2.0, in1=over_positions(mean_c),
-            op0=ALU.mult, op1=ALU.subtract,
-        )
-        nc.vector.tensor_tensor(out=shift_c, in0=shift_c, in1=over_positions(gain_c), op=ALU.mult)
-        nc.vector.tensor_tensor(out=shift_c, in0=shift_c, in1=over_positions(beta_c), op=ALU.add)
-
-        spread = keep.tile([P, POSITIONS + 1, FILTERS], F32)
-        for v in range(POSITIONS + 1):
+        spread = keep.tile([P, 1 + POSITIONS, FILTERS], F32)
+        for v in range(1 + POSITIONS):
             spread_ps = setup_psum.tile([P, FILTERS], F32, tag="setup", name="spread_ps")
             for c in range(CHUNKS):
                 col = CHUNKS * v + c
@@ -181,7 +157,10 @@ def tile_residualblock5_pa_e_kernel(
                     folded[:, col : col + 1].to_broadcast([P, P]),
                     ident_f32[:],
                 )
-            nc.scalar.copy(out=spread[:, v, :], in_=spread_ps[:])
+            if v % 2 == 0:
+                nc.scalar.copy(out=spread[:, v, :], in_=spread_ps[:])
+            else:
+                nc.vector.tensor_copy(out=spread[:, v, :], in_=spread_ps[:])
 
         for position in range(POSITIONS):
             acc = acc_psum.tile([P, FILTERS], F32)
@@ -192,15 +171,15 @@ def tile_residualblock5_pa_e_kernel(
                     out=acc[:],
                     lhsT=x_codes[:, P * x_pos : P * (x_pos + 1)].bitcast(FP8X4),
                     lhsT_scale=x_scales[:, P * x_pos : P * (x_pos + 1)],
-                    rhs=weights[(tap, position)][:].bitcast(FP8X4),
+                    rhs=weights[position][:, tap, :].bitcast(FP8X4),
                     rhs_scale=planes[offset:P, FILTERS * slot : FILTERS * (slot + 1)],
                     start=(tap == 0),
                     stop=(tap == TAPS - 1),
                 )
             z = work.tile([P, FILTERS], F32)
-            nc.vector.tensor_tensor(out=z[:], in0=acc[:], in1=spread[:, POSITIONS, :], op=ALU.mult)
-            nc.vector.tensor_tensor(out=z[:], in0=z[:], in1=spread[:, position, :], op=ALU.add)
+            nc.vector.tensor_tensor(out=z[:], in0=acc[:], in1=spread[:, 0, :], op=ALU.mult)
+            nc.vector.tensor_tensor(out=z[:], in0=z[:], in1=spread[:, 1 + position, :], op=ALU.add)
             nc.vector.scalar_tensor_tensor(
                 out=z[:], in0=z[:], scalar=LEAKY_ALPHA, in1=z[:], op0=ALU.mult, op1=ALU.max
             )
-            nc.scalar.dma_start(out=out[:, position, :], in_=z[:])
+            nc.sync.dma_start(out=out[:, position, :], in_=z[:])

@@ -29,7 +29,7 @@ FLOPS = 2 * P * POSITIONS * TAPS * CHANNELS * FILTERS
 
 def plane_place(tap, position):
     matrix = POSITIONS * tap + position
-    return matrix % SLOTS, 4 * (matrix // SLOTS)
+    return matrix // PLANES_PER_SLOT, 4 * (matrix % PLANES_PER_SLOT)
 
 
 def tile_residualblock5_pa_e_kernel(
@@ -74,7 +74,7 @@ def tile_residualblock5_pa_e_kernel(
         nc.sync.dma_start(out=x_sb[:], in_=x.rearrange("b l c -> b (l c)"))
 
         scale_rows = k1_scales.rearrange(
-            "(j s) (q r) n -> q r j s n", j=PLANES_PER_SLOT, r=4
+            "(s j) (q r) n -> q r j s n", j=PLANES_PER_SLOT, r=4
         )
         for r in range(4):
             for quadrant in range(QUADRANTS):

@@ -23,13 +23,15 @@ CHUNKS = FILTERS // P
 PLANES_PER_SLOT = 4
 SLOTS = TAPS * POSITIONS // PLANES_PER_SLOT
 QUADRANTS = 4
+POSITIONS_ON_SYNC = 2
 
 FLOPS = 2 * P * POSITIONS * TAPS * CHANNELS * FILTERS
 
 
 def plane_place(tap, position):
-    matrix = POSITIONS * tap + position
-    return matrix // PLANES_PER_SLOT, 4 * (matrix % PLANES_PER_SLOT)
+    if tap < PLANES_PER_SLOT:
+        return position, 4 * tap
+    return POSITIONS + position // PLANES_PER_SLOT, 4 * (position % PLANES_PER_SLOT)
 
 
 def tile_residualblock5_pa_e_kernel(
@@ -73,16 +75,29 @@ def tile_residualblock5_pa_e_kernel(
 
         nc.sync.dma_start(out=x_sb[:], in_=x.rearrange("b l c -> b (l c)"))
 
-        scale_rows = k1_scales.rearrange(
-            "(s j) (q r) n -> q r j s n", j=PLANES_PER_SLOT, r=4
-        )
-        for r in range(4):
+        scales_by_position = k1_scales.rearrange("(i l) q n -> l i q n", l=POSITIONS)
+
+        def load_slot(queue, view, slot):
             for quadrant in range(QUADRANTS):
-                first = 32 * quadrant + r
-                nc.sync.dma_start(
-                    out=planes[first : first + 16 : 4, :].bitcast(I32),
-                    in_=scale_rows[quadrant, r].bitcast(I32),
+                rows = slice(4 * quadrant, 4 * quadrant + 4)
+                if slot < POSITIONS:
+                    source = scales_by_position[slot, 0:PLANES_PER_SLOT, rows, :]
+                else:
+                    first = PLANES_PER_SLOT * slot
+                    source = k1_scales[first : first + PLANES_PER_SLOT, rows, :]
+                queue.dma_start(
+                    out=planes[
+                        32 * quadrant : 32 * quadrant + 16, FILTERS * slot : FILTERS * (slot + 1)
+                    ].bitcast(view),
+                    in_=source.bitcast(view),
                 )
+
+        for slot in (POSITIONS, POSITIONS + 1):
+            load_slot(nc.sync, I32, slot)
+        for slot in range(POSITIONS_ON_SYNC):
+            load_slot(nc.sync, I32, slot)
+        for slot in range(POSITIONS_ON_SYNC, POSITIONS):
+            load_slot(nc.gpsimd, F32, slot)
 
         words_by_position = k1_words.rearrange("(i l) p n t -> l p i (n t)", l=POSITIONS)
         for position in range(POSITIONS):

@@ -23,15 +23,13 @@ CHUNKS = FILTERS // P
 PLANES_PER_SLOT = 4
 SLOTS = TAPS * POSITIONS // PLANES_PER_SLOT
 QUADRANTS = 4
-POSITIONS_ON_SYNC = 2
 
 FLOPS = 2 * P * POSITIONS * TAPS * CHANNELS * FILTERS
 
 
 def plane_place(tap, position):
-    if tap < PLANES_PER_SLOT:
-        return position, 4 * tap
-    return POSITIONS + position // PLANES_PER_SLOT, 4 * (position % PLANES_PER_SLOT)
+    matrix = POSITIONS * tap + position
+    return matrix // PLANES_PER_SLOT, 4 * (matrix % PLANES_PER_SLOT)
 
 
 def tile_residualblock5_pa_e_kernel(
@@ -50,8 +48,12 @@ def tile_residualblock5_pa_e_kernel(
         x_codes = keep.tile([P, POSITIONS * P], I32, align_bytes=64)
         x_scales = keep.tile([P, POSITIONS * P], U8, align_bytes=64)
         planes = keep.tile([P, SLOTS * FILTERS], U8, align_bytes=64)
-        weights = [
-            keep.tile([P, TAPS, FILTERS], I32, align_bytes=64, name="w%d" % position)
+        first_taps = [
+            keep.tile([P, TAPS - 1, FILTERS], I32, align_bytes=64, name="first_taps%d" % position)
+            for position in range(POSITIONS)
+        ]
+        last_tap = [
+            keep.tile([P, FILTERS], I32, align_bytes=64, name="last_tap%d" % position)
             for position in range(POSITIONS)
         ]
         vec_rows = keep.tile([P, P], BF16)
@@ -75,34 +77,26 @@ def tile_residualblock5_pa_e_kernel(
 
         nc.sync.dma_start(out=x_sb[:], in_=x.rearrange("b l c -> b (l c)"))
 
-        scales_by_position = k1_scales.rearrange("(i l) q n -> l i q n", l=POSITIONS)
-
-        def load_slot(queue, view, slot):
+        scale_rows = k1_scales.rearrange(
+            "(s j) (q r) n -> q r j s n", j=PLANES_PER_SLOT, r=4
+        )
+        for r in range(4):
             for quadrant in range(QUADRANTS):
-                rows = slice(4 * quadrant, 4 * quadrant + 4)
-                if slot < POSITIONS:
-                    source = scales_by_position[slot, 0:PLANES_PER_SLOT, rows, :]
-                else:
-                    first = PLANES_PER_SLOT * slot
-                    source = k1_scales[first : first + PLANES_PER_SLOT, rows, :]
-                queue.dma_start(
-                    out=planes[
-                        32 * quadrant : 32 * quadrant + 16, FILTERS * slot : FILTERS * (slot + 1)
-                    ].bitcast(view),
-                    in_=source.bitcast(view),
+                first = 32 * quadrant + r
+                nc.sync.dma_start(
+                    out=planes[first : first + 16 : 4, :].bitcast(I32),
+                    in_=scale_rows[quadrant, r].bitcast(I32),
                 )
-
-        for slot in (POSITIONS, POSITIONS + 1):
-            load_slot(nc.sync, I32, slot)
-        for slot in range(POSITIONS_ON_SYNC):
-            load_slot(nc.sync, I32, slot)
-        for slot in range(POSITIONS_ON_SYNC, POSITIONS):
-            load_slot(nc.gpsimd, F32, slot)
 
         words_by_position = k1_words.rearrange("(i l) p n t -> l p i (n t)", l=POSITIONS)
         for position in range(POSITIONS):
             nc.sync.dma_start(
-                out=weights[position][:], in_=words_by_position[position].bitcast(I32)
+                out=first_taps[position][:],
+                in_=words_by_position[position, :, 0 : TAPS - 1, :].bitcast(I32),
+            )
+            nc.sync.dma_start(
+                out=last_tap[position][:],
+                in_=words_by_position[position, :, TAPS - 1, :].bitcast(I32),
             )
 
         nc.vector.tensor_copy(out=ident_bf16[:], in_=ident_f32[:])
@@ -182,11 +176,15 @@ def tile_residualblock5_pa_e_kernel(
             for tap in range(TAPS):
                 x_pos = (position - STEP[tap]) % POSITIONS
                 slot, offset = plane_place(tap, position)
+                if tap < TAPS - 1:
+                    words = first_taps[position][:, tap, :]
+                else:
+                    words = last_tap[position][:]
                 nc.tensor.matmul_mx(
                     out=acc[:],
                     lhsT=x_codes[:, P * x_pos : P * (x_pos + 1)].bitcast(FP8X4),
                     lhsT_scale=x_scales[:, P * x_pos : P * (x_pos + 1)],
-                    rhs=weights[position][:, tap, :].bitcast(FP8X4),
+                    rhs=words.bitcast(FP8X4),
                     rhs_scale=planes[offset:P, FILTERS * slot : FILTERS * (slot + 1)],
                     start=(tap == 0),
                     stop=(tap == TAPS - 1),

@@ -83,10 +83,16 @@ def tile_residualblock5_pa_e_kernel(
         for r in range(4):
             for quadrant in range(QUADRANTS):
                 first = 32 * quadrant + r
-                nc.sync.dma_start(
-                    out=planes[first : first + 16 : 4, :].bitcast(I32),
-                    in_=scale_rows[quadrant, r].bitcast(I32),
-                )
+                if r < 2:
+                    nc.sync.dma_start(
+                        out=planes[first : first + 16 : 4, :].bitcast(I32),
+                        in_=scale_rows[quadrant, r].bitcast(I32),
+                    )
+                else:
+                    nc.gpsimd.dma_start(
+                        out=planes[first : first + 16 : 4, :].bitcast(F32),
+                        in_=scale_rows[quadrant, r].bitcast(F32),
+                    )
 
         words_by_position = k1_words.rearrange("(i l) p n t -> l p i (n t)", l=POSITIONS)
         for position in range(POSITIONS):

@@ -196,9 +196,18 @@ def tile_residualblock5_pa_e_kernel(
                     stop=(tap == TAPS - 1),
                 )
             z = work.tile([P, FILTERS], F32)
-            nc.vector.tensor_tensor(out=z[:], in0=acc[:], in1=spread[:, 0, :], op=ALU.mult)
-            nc.vector.tensor_tensor(out=z[:], in0=z[:], in1=spread[:, 1 + position, :], op=ALU.add)
-            nc.vector.scalar_tensor_tensor(
-                out=z[:], in0=z[:], scalar=LEAKY_ALPHA, in1=z[:], op0=ALU.mult, op1=ALU.max
-            )
+            halves = [slice(h * FILTERS // 2, (h + 1) * FILTERS // 2) for h in range(2)]
+            for cols in halves:
+                nc.vector.tensor_tensor(
+                    out=z[:, cols], in0=acc[:, cols], in1=spread[:, 0, cols], op=ALU.mult
+                )
+            for cols in halves:
+                nc.vector.tensor_tensor(
+                    out=z[:, cols], in0=z[:, cols], in1=spread[:, 1 + position, cols], op=ALU.add
+                )
+            for cols in halves:
+                nc.vector.scalar_tensor_tensor(
+                    out=z[:, cols], in0=z[:, cols], scalar=LEAKY_ALPHA, in1=z[:, cols],
+                    op0=ALU.mult, op1=ALU.max,
+                )
             nc.sync.dma_start(out=out[:, position, :], in_=z[:])

@@ -80,19 +80,17 @@ def tile_residualblock5_pa_e_kernel(
         scale_rows = k1_scales.rearrange(
             "(s j) (q r) n -> q r j s n", j=PLANES_PER_SLOT, r=4
         )
-        for r in range(4):
+        def load_scale_rows(queue, view, quadrant, r):
+            first = 32 * quadrant + r
+            queue.dma_start(
+                out=planes[first : first + 16 : 4, :].bitcast(view),
+                in_=scale_rows[quadrant, r].bitcast(view),
+            )
+
+        for r in (2, 3):
             for quadrant in range(QUADRANTS):
-                first = 32 * quadrant + r
-                if r < 2:
-                    nc.sync.dma_start(
-                        out=planes[first : first + 16 : 4, :].bitcast(I32),
-                        in_=scale_rows[quadrant, r].bitcast(I32),
-                    )
-                else:
-                    nc.gpsimd.dma_start(
-                        out=planes[first : first + 16 : 4, :].bitcast(F32),
-                        in_=scale_rows[quadrant, r].bitcast(F32),
-                    )
+                load_scale_rows(nc.gpsimd, F32, quadrant, r)
+        on_sync = [(quadrant, r) for r in (0, 1) for quadrant in range(QUADRANTS)]
 
         words_by_position = k1_words.rearrange("(i l) p n t -> l p i (n t)", l=POSITIONS)
         for position in range(POSITIONS):
@@ -100,10 +98,14 @@ def tile_residualblock5_pa_e_kernel(
                 out=first_taps[position][:],
                 in_=words_by_position[position, :, 0 : TAPS - 1, :].bitcast(I32),
             )
+            for quadrant, r in on_sync[4 * position : 4 * position + 2]:
+                load_scale_rows(nc.sync, I32, quadrant, r)
             nc.sync.dma_start(
                 out=last_tap[position][:],
                 in_=words_by_position[position, :, TAPS - 1, :].bitcast(I32),
             )
+            for quadrant, r in on_sync[4 * position + 2 : 4 * position + 4]:
+                load_scale_rows(nc.sync, I32, quadrant, r)
 
         nc.vector.tensor_copy(out=ident_bf16[:], in_=ident_f32[:])
 

@@ -43,17 +43,17 @@ def tile_residualblock5_pa_e_kernel(
         setup_psum = ctx.enter_context(tc.psum_pool(name="setup_psum", bufs=4))
         acc_psum = ctx.enter_context(tc.psum_pool(name="acc_psum", bufs=4))
 
-        x_sb = keep.tile([P, POSITIONS * CHANNELS], BF16)
+        x_sb = keep.tile([P, POSITIONS * CHANNELS], BF16, align_bytes=256)
         grouped = keep.tile([P, POSITIONS * CHANNELS], BF16, align_bytes=64)
         x_codes = keep.tile([P, POSITIONS * P], I32, align_bytes=64)
         x_scales = keep.tile([P, POSITIONS * P], U8, align_bytes=64)
-        planes = keep.tile([P, SLOTS * FILTERS], U8, align_bytes=64)
+        planes = keep.tile([P, SLOTS * FILTERS], U8, align_bytes=256)
         first_taps = [
-            keep.tile([P, TAPS - 1, FILTERS], I32, align_bytes=64, name="first_taps%d" % position)
+            keep.tile([P, TAPS - 1, FILTERS], I32, align_bytes=256, name="first_taps%d" % position)
             for position in range(POSITIONS)
         ]
         last_tap = [
-            keep.tile([P, FILTERS], I32, align_bytes=64, name="last_tap%d" % position)
+            keep.tile([P, FILTERS], I32, align_bytes=256, name="last_tap%d" % position)
             for position in range(POSITIONS)
         ]
         vec_rows = keep.tile([P, P], BF16)
@@ -197,7 +197,7 @@ def tile_residualblock5_pa_e_kernel(
                     start=(tap == 0),
                     stop=(tap == TAPS - 1),
                 )
-            z = work.tile([P, FILTERS], F32)
+            z = work.tile([P, FILTERS], F32, align_bytes=256)
             halves = [slice(h * FILTERS // 2, (h + 1) * FILTERS // 2) for h in range(2)]
             for cols in halves:
                 nc.vector.tensor_tensor(

@@ -24,6 +24,8 @@ PLANES_PER_SLOT = 4
 SLOTS = TAPS * POSITIONS // PLANES_PER_SLOT
 QUADRANTS = 4
 
+STORES = ((0, 3), (4, 5), (6, 6), (7, 7))
+
 FLOPS = 2 * P * POSITIONS * TAPS * CHANNELS * FILTERS
 
 
@@ -39,7 +41,6 @@ def tile_residualblock5_pa_e_kernel(
     with ExitStack() as ctx:
         ctx.enter_context(tc.manual_schedule())
         keep = ctx.enter_context(tc.tile_pool(name="keep", bufs=1))
-        work = ctx.enter_context(tc.tile_pool(name="work", bufs=POSITIONS))
         setup_psum = ctx.enter_context(tc.psum_pool(name="setup_psum", bufs=4))
         acc_psum = ctx.enter_context(tc.psum_pool(name="acc_psum", bufs=4))
 
@@ -56,6 +57,7 @@ def tile_residualblock5_pa_e_kernel(
             keep.tile([P, FILTERS], I32, align_bytes=256, name="last_tap%d" % position)
             for position in range(POSITIONS)
         ]
+        z_all = keep.tile([P, POSITIONS * FILTERS], F32, align_bytes=256)
         vec_rows = keep.tile([P, P], BF16)
         ident_f32 = keep.tile([P, P], F32)
         ident_bf16 = keep.tile([P, P], BF16)
@@ -179,6 +181,7 @@ def tile_residualblock5_pa_e_kernel(
             else:
                 nc.vector.tensor_copy(out=spread[:, v, :], in_=spread_ps[:])
 
+        out_rows = out.rearrange("b l f -> b (l f)")
         for position in range(POSITIONS):
             acc = acc_psum.tile([P, FILTERS], F32)
             for tap in range(TAPS):
@@ -197,7 +200,7 @@ def tile_residualblock5_pa_e_kernel(
                     start=(tap == 0),
                     stop=(tap == TAPS - 1),
                 )
-            z = work.tile([P, FILTERS], F32, align_bytes=256)
+            z = z_all[:, FILTERS * position : FILTERS * (position + 1)]
             halves = [slice(h * FILTERS // 2, (h + 1) * FILTERS // 2) for h in range(2)]
             for cols in halves:
                 nc.vector.tensor_tensor(
@@ -212,4 +215,9 @@ def tile_residualblock5_pa_e_kernel(
                     out=z[:, cols], in0=z[:, cols], scalar=LEAKY_ALPHA, in1=z[:, cols],
                     op0=ALU.mult, op1=ALU.max,
                 )
-            nc.sync.dma_start(out=out[:, position, :], in_=z[:])
+            for first, last in STORES:
+                if last == position:
+                    nc.sync.dma_start(
+                        out=out_rows[:, FILTERS * first : FILTERS * (last + 1)],
+                        in_=z_all[:, FILTERS * first : FILTERS * (last + 1)],
+                    )

@@ -89,10 +89,10 @@ def tile_residualblock5_pa_e_kernel(
                 in_=scale_rows[quadrant, r].bitcast(view),
             )
 
-        for r in (2, 3):
-            for quadrant in range(QUADRANTS):
+        for r in range(4):
+            for quadrant in (2, 3):
                 load_scale_rows(nc.gpsimd, F32, quadrant, r)
-        on_sync = [(quadrant, r) for r in (0, 1) for quadrant in range(QUADRANTS)]
+        on_sync = [(quadrant, r) for r in range(4) for quadrant in (0, 1)]
 
         words_by_position = k1_words.rearrange("(i l) p n t -> l p i (n t)", l=POSITIONS)
         for position in range(POSITIONS):

@@ -24,7 +24,7 @@ PLANES_PER_SLOT = 4
 SLOTS = TAPS * POSITIONS // PLANES_PER_SLOT
 QUADRANTS = 4
 
-STORES = ((0, 3), (4, 5), (6, 6), (7, 7))
+STORES = ((0, 3), (4, 5), (6, 6))
 
 FLOPS = 2 * P * POSITIONS * TAPS * CHANNELS * FILTERS
 
@@ -183,7 +183,12 @@ def tile_residualblock5_pa_e_kernel(
 
         out_rows = out.rearrange("b l f -> b (l f)")
         for position in range(POSITIONS):
-            acc = acc_psum.tile([P, FILTERS], F32)
+            parts = 2 if position == POSITIONS - 1 else 1
+            width = FILTERS // parts
+            accs = []
+            for part in range(parts):
+                acc = acc_psum.tile([P, width], F32, tag="acc", name="acc")
+                accs.append(acc)
             for tap in range(TAPS):
                 x_pos = (position - STEP[tap]) % POSITIONS
                 slot, offset = plane_place(tap, position)
@@ -191,20 +196,26 @@ def tile_residualblock5_pa_e_kernel(
                     words = first_taps[position][:, tap, :]
                 else:
                     words = last_tap[position][:]
-                nc.tensor.matmul_mx(
-                    out=acc[:],
-                    lhsT=x_codes[:, P * x_pos : P * (x_pos + 1)].bitcast(FP8X4),
-                    lhsT_scale=x_scales[:, P * x_pos : P * (x_pos + 1)],
-                    rhs=words.bitcast(FP8X4),
-                    rhs_scale=planes[offset:P, FILTERS * slot : FILTERS * (slot + 1)],
-                    start=(tap == 0),
-                    stop=(tap == TAPS - 1),
-                )
+                for part in range(parts):
+                    first = width * part
+                    nc.tensor.matmul_mx(
+                        out=accs[part][:],
+                        lhsT=x_codes[:, P * x_pos : P * (x_pos + 1)].bitcast(FP8X4),
+                        lhsT_scale=x_scales[:, P * x_pos : P * (x_pos + 1)],
+                        rhs=words[:, first : first + width].bitcast(FP8X4),
+                        rhs_scale=planes[
+                            offset:P, FILTERS * slot + first : FILTERS * slot + first + width
+                        ],
+                        start=(tap == 0),
+                        stop=(tap == TAPS - 1),
+                    )
             z = z_all[:, FILTERS * position : FILTERS * (position + 1)]
             halves = [slice(h * FILTERS // 2, (h + 1) * FILTERS // 2) for h in range(2)]
             for cols in halves:
+                acc = accs[cols.start // width]
+                acc_cols = slice(cols.start % width, cols.start % width + FILTERS // 2)
                 nc.vector.tensor_tensor(
-                    out=z[:, cols], in0=acc[:, cols], in1=spread[:, 0, cols], op=ALU.mult
+                    out=z[:, cols], in0=acc[:, acc_cols], in1=spread[:, 0, cols], op=ALU.mult
                 )
             for cols in halves:
                 nc.vector.tensor_tensor(
@@ -215,6 +226,11 @@ def tile_residualblock5_pa_e_kernel(
                     out=z[:, cols], in0=z[:, cols], scalar=LEAKY_ALPHA, in1=z[:, cols],
                     op0=ALU.mult, op1=ALU.max,
                 )
+                if position == POSITIONS - 1:
+                    nc.sync.dma_start(
+                        out=out_rows[:, FILTERS * position + cols.start : FILTERS * position + cols.stop],
+                        in_=z[:, cols],
+                    )
             for first, last in STORES:
                 if last == position:
                     nc.sync.dma_start(

@@ -26,6 +26,13 @@ QUADRANTS = 4
 
 STORES = ((0, 3), (4, 5), (6, 6))
 
+
+def tap_groups(position):
+    if position == POSITIONS - 1:
+        return [(tap, tap) for tap in range(TAPS)]
+    return [(0, TAPS - 2), (TAPS - 1, TAPS - 1)]
+
+
 FLOPS = 2 * P * POSITIONS * TAPS * CHANNELS * FILTERS
 
 
@@ -49,14 +56,16 @@ def tile_residualblock5_pa_e_kernel(
         x_codes = keep.tile([P, POSITIONS * P], I32, align_bytes=64)
         x_scales = keep.tile([P, POSITIONS * P], U8, align_bytes=64)
         planes = keep.tile([P, SLOTS * FILTERS], U8, align_bytes=256)
-        first_taps = [
-            keep.tile([P, TAPS - 1, FILTERS], I32, align_bytes=256, name="first_taps%d" % position)
-            for position in range(POSITIONS)
-        ]
-        last_tap = [
-            keep.tile([P, FILTERS], I32, align_bytes=256, name="last_tap%d" % position)
-            for position in range(POSITIONS)
-        ]
+        weights = []
+        for position in range(POSITIONS):
+            tiles = []
+            for first, last in tap_groups(position):
+                words = keep.tile(
+                    [P, last - first + 1, FILTERS], I32, align_bytes=256,
+                    name="words%d_%d" % (position, first),
+                )
+                tiles.append(words)
+            weights.append(tiles)
         z_all = keep.tile([P, POSITIONS * FILTERS], F32, align_bytes=256)
         vec_rows = keep.tile([P, P], BF16)
         ident_f32 = keep.tile([P, P], F32)
@@ -96,18 +105,14 @@ def tile_residualblock5_pa_e_kernel(
 
         words_by_position = k1_words.rearrange("(i l) p n t -> l p i (n t)", l=POSITIONS)
         for position in range(POSITIONS):
-            nc.sync.dma_start(
-                out=first_taps[position][:],
-                in_=words_by_position[position, :, 0 : TAPS - 1, :].bitcast(I32),
-            )
-            for quadrant, r in on_sync[4 * position : 4 * position + 2]:
-                load_scale_rows(nc.sync, I32, quadrant, r)
-            nc.sync.dma_start(
-                out=last_tap[position][:],
-                in_=words_by_position[position, :, TAPS - 1, :].bitcast(I32),
-            )
-            for quadrant, r in on_sync[4 * position + 2 : 4 * position + 4]:
-                load_scale_rows(nc.sync, I32, quadrant, r)
+            for tile, (first, last) in zip(weights[position], tap_groups(position)):
+                nc.sync.dma_start(
+                    out=tile[:],
+                    in_=words_by_position[position, :, first : last + 1, :].bitcast(I32),
+                )
+                for quadrant, r in on_sync[:2]:
+                    load_scale_rows(nc.sync, I32, quadrant, r)
+                on_sync = on_sync[2:]
 
         nc.vector.tensor_copy(out=ident_bf16[:], in_=ident_f32[:])
 
@@ -192,10 +197,9 @@ def tile_residualblock5_pa_e_kernel(
             for tap in range(TAPS):
                 x_pos = (position - STEP[tap]) % POSITIONS
                 slot, offset = plane_place(tap, position)
-                if tap < TAPS - 1:
-                    words = first_taps[position][:, tap, :]
-                else:
-                    words = last_tap[position][:]
+                for tile, (first, last) in zip(weights[position], tap_groups(position)):
+                    if first <= tap <= last:
+                        words = tile[:, tap - first, :]
                 for part in range(parts):
                     first = width * part
                     nc.tensor.matmul_mx(

@@ -18,6 +18,7 @@ TAPS = 5
 STEP = (0, 0, 1, -1, 2)
 BN_EPS = 1e-3
 LEAKY_ALPHA = 0.3
+SPLIT_TAP = 2
 CHUNKS = FILTERS // P
 
 PLANES_PER_SLOT = 4
@@ -27,10 +28,21 @@ QUADRANTS = 4
 STORES = ((0, 3), (4, 5), (6, 6))
 
 
-def tap_groups(position):
-    if position == POSITIONS - 1:
-        return [(tap, tap) for tap in range(TAPS)]
-    return [(0, TAPS - 2), (TAPS - 1, TAPS - 1)]
+def weight_loads(position):
+    last = TAPS - 1
+    if position < POSITIONS - 1:
+        return [(0, last - 1, 0, FILTERS - 1), (last, last, 0, FILTERS - 1)]
+    loads = [(tap, tap, 0, FILTERS - 1) for tap in range(SPLIT_TAP)]
+    loads.append((SPLIT_TAP, last, 0, FILTERS // 2 - 1))
+    loads.append((SPLIT_TAP, last - 1, FILTERS // 2, FILTERS - 1))
+    loads.append((last, last, FILTERS // 2, FILTERS - 1))
+    return loads
+
+
+def parts_of(position):
+    if position < POSITIONS - 1:
+        return [(0, FILTERS)]
+    return [(0, FILTERS // 2), (FILTERS // 2, FILTERS // 2)]
 
 
 FLOPS = 2 * P * POSITIONS * TAPS * CHANNELS * FILTERS
@@ -59,10 +71,10 @@ def tile_residualblock5_pa_e_kernel(
         weights = []
         for position in range(POSITIONS):
             tiles = []
-            for first, last in tap_groups(position):
+            for first, last, left, right in weight_loads(position):
                 words = keep.tile(
-                    [P, last - first + 1, FILTERS], I32, align_bytes=256,
-                    name="words%d_%d" % (position, first),
+                    [P, last - first + 1, right - left + 1], I32, align_bytes=256,
+                    name="words%d_%d_%d" % (position, first, left),
                 )
                 tiles.append(words)
             weights.append(tiles)
@@ -105,10 +117,12 @@ def tile_residualblock5_pa_e_kernel(
 
         words_by_position = k1_words.rearrange("(i l) p n t -> l p i (n t)", l=POSITIONS)
         for position in range(POSITIONS):
-            for tile, (first, last) in zip(weights[position], tap_groups(position)):
+            for tile, (first, last, left, right) in zip(weights[position], weight_loads(position)):
                 nc.sync.dma_start(
                     out=tile[:],
-                    in_=words_by_position[position, :, first : last + 1, :].bitcast(I32),
+                    in_=words_by_position[
+                        position, :, first : last + 1, 4 * left : 4 * (right + 1)
+                    ].bitcast(I32),
                 )
                 for quadrant, r in on_sync[:2]:
                     load_scale_rows(nc.sync, I32, quadrant, r)
@@ -188,53 +202,47 @@ def tile_residualblock5_pa_e_kernel(
 
         out_rows = out.rearrange("b l f -> b (l f)")
         for position in range(POSITIONS):
-            parts = 2 if position == POSITIONS - 1 else 1
-            width = FILTERS // parts
+            parts = parts_of(position)
             accs = []
-            for part in range(parts):
+            for part, width in parts:
                 acc = acc_psum.tile([P, width], F32, tag="acc", name="acc")
                 accs.append(acc)
-            for tap in range(TAPS):
-                x_pos = (position - STEP[tap]) % POSITIONS
-                slot, offset = plane_place(tap, position)
-                for tile, (first, last) in zip(weights[position], tap_groups(position)):
-                    if first <= tap <= last:
-                        words = tile[:, tap - first, :]
-                for part in range(parts):
-                    first = width * part
-                    nc.tensor.matmul_mx(
-                        out=accs[part][:],
-                        lhsT=x_codes[:, P * x_pos : P * (x_pos + 1)].bitcast(FP8X4),
-                        lhsT_scale=x_scales[:, P * x_pos : P * (x_pos + 1)],
-                        rhs=words[:, first : first + width].bitcast(FP8X4),
-                        rhs_scale=planes[
-                            offset:P, FILTERS * slot + first : FILTERS * slot + first + width
-                        ],
-                        start=(tap == 0),
-                        stop=(tap == TAPS - 1),
+            for tile, (first, last, left, right) in zip(weights[position], weight_loads(position)):
+                for tap in range(first, last + 1):
+                    x_pos = (position - STEP[tap]) % POSITIONS
+                    slot, offset = plane_place(tap, position)
+                    for acc, (part, width) in zip(accs, parts):
+                        if part < left or part > right:
+                            continue
+                        column = FILTERS * slot + part
+                        nc.tensor.matmul_mx(
+                            out=acc[:],
+                            lhsT=x_codes[:, P * x_pos : P * (x_pos + 1)].bitcast(FP8X4),
+                            lhsT_scale=x_scales[:, P * x_pos : P * (x_pos + 1)],
+                            rhs=tile[:, tap - first, part - left : part - left + width].bitcast(FP8X4),
+                            rhs_scale=planes[offset:P, column : column + width],
+                            start=(tap == 0),
+                            stop=(tap == TAPS - 1),
+                        )
+            for acc, (part, width) in zip(accs, parts):
+                z = z_all[:, FILTERS * position + part : FILTERS * position + part + width]
+                half = width // 2
+                halves = [(slice(h, h + half), slice(part + h, part + h + half)) for h in (0, half)]
+                for here, cols in halves:
+                    nc.vector.tensor_tensor(
+                        out=z[:, here], in0=acc[:, here], in1=spread[:, 0, cols], op=ALU.mult
                     )
-            z = z_all[:, FILTERS * position : FILTERS * (position + 1)]
-            halves = [slice(h * FILTERS // 2, (h + 1) * FILTERS // 2) for h in range(2)]
-            for cols in halves:
-                acc = accs[cols.start // width]
-                acc_cols = slice(cols.start % width, cols.start % width + FILTERS // 2)
-                nc.vector.tensor_tensor(
-                    out=z[:, cols], in0=acc[:, acc_cols], in1=spread[:, 0, cols], op=ALU.mult
-                )
-            for cols in halves:
-                nc.vector.tensor_tensor(
-                    out=z[:, cols], in0=z[:, cols], in1=spread[:, 1 + position, cols], op=ALU.add
-                )
-            for cols in halves:
-                nc.vector.scalar_tensor_tensor(
-                    out=z[:, cols], in0=z[:, cols], scalar=LEAKY_ALPHA, in1=z[:, cols],
-                    op0=ALU.mult, op1=ALU.max,
-                )
-                if position == POSITIONS - 1:
-                    nc.sync.dma_start(
-                        out=out_rows[:, FILTERS * position + cols.start : FILTERS * position + cols.stop],
-                        in_=z[:, cols],
+                for here, cols in halves:
+                    nc.vector.tensor_tensor(
+                        out=z[:, here], in0=z[:, here], in1=spread[:, 1 + position, cols], op=ALU.add
                     )
+                for here, cols in halves:
+                    nc.vector.scalar_tensor_tensor(
+                        out=z[:, here], in0=z[:, here], scalar=LEAKY_ALPHA, in1=z[:, here],
+                        op0=ALU.mult, op1=ALU.max,
+                    )
+                if len(parts) > 1:
+                    nc.sync.dma_start(out=out[:, position, part : part + width], in_=z)
             for first, last in STORES:
                 if last == position:
                     nc.sync.dma_start(

from contextlib import ExitStack

import concourse.mybir as mybir
from concourse.masks import make_identity

F32 = mybir.dt.float32
BF16 = mybir.dt.bfloat16
I32 = mybir.dt.int32
U8 = mybir.dt.uint8
FP8X4 = mybir.dt.float8_e4m3fn_x4
ALU = mybir.AluOpType

P = 128
POSITIONS = 8
CHANNELS = 512
FILTERS = 512
TAPS = 5
STEP = (0, 0, 1, -1, 2)
BN_EPS = 1e-3
LEAKY_ALPHA = 0.3
SPLIT_TAP = 2
CHUNKS = FILTERS // P

PLANES_PER_SLOT = 4
SLOTS = TAPS * POSITIONS // PLANES_PER_SLOT
QUADRANTS = 4

STORES = ((0, 3), (4, 5), (6, 6))


def weight_loads(position):
    last = TAPS - 1
    if position < POSITIONS - 1:
        return [(0, last - 1, 0, FILTERS - 1), (last, last, 0, FILTERS - 1)]
    loads = [(tap, tap, 0, FILTERS - 1) for tap in range(SPLIT_TAP)]
    loads.append((SPLIT_TAP, last, 0, FILTERS // 2 - 1))
    loads.append((SPLIT_TAP, last - 1, FILTERS // 2, FILTERS - 1))
    loads.append((last, last, FILTERS // 2, FILTERS - 1))
    return loads


def parts_of(position):
    if position < POSITIONS - 1:
        return [(0, FILTERS)]
    return [(0, FILTERS // 2), (FILTERS // 2, FILTERS // 2)]


FLOPS = 2 * P * POSITIONS * TAPS * CHANNELS * FILTERS


def plane_place(tap, position):
    matrix = POSITIONS * tap + position
    return matrix // PLANES_PER_SLOT, 4 * (matrix % PLANES_PER_SLOT)


def tile_residualblock5_pa_e_kernel(
    tc, x, k1_words, k1_scales, b1, gamma1, beta1, mean1, var1, out
):
    nc = tc.nc
    with ExitStack() as ctx:
        ctx.enter_context(tc.manual_schedule())
        keep = ctx.enter_context(tc.tile_pool(name="keep", bufs=1))
        setup_psum = ctx.enter_context(tc.psum_pool(name="setup_psum", bufs=4))
        acc_psum = ctx.enter_context(tc.psum_pool(name="acc_psum", bufs=4))

        x_sb = keep.tile([P, POSITIONS * CHANNELS], BF16, align_bytes=256)
        grouped = keep.tile([P, POSITIONS * CHANNELS], BF16, align_bytes=64)
        x_codes = keep.tile([P, POSITIONS * P], I32, align_bytes=64)
        x_scales = keep.tile([P, POSITIONS * P], U8, align_bytes=64)
        planes = keep.tile([P, SLOTS * FILTERS], U8, align_bytes=256)
        weights = []
        for position in range(POSITIONS):
            tiles = []
            for first, last, left, right in weight_loads(position):
                words = keep.tile(
                    [P, last - first + 1, right - left + 1], I32, align_bytes=256,
                    name="words%d_%d_%d" % (position, first, left),
                )
                tiles.append(words)
            weights.append(tiles)
        z_all = keep.tile([P, POSITIONS * FILTERS], F32, align_bytes=256)
        vec_rows = keep.tile([P, P], BF16)
        ident_f32 = keep.tile([P, P], F32)
        ident_bf16 = keep.tile([P, P], BF16)

        make_identity(nc, ident_f32[:])
        nc.vector.memset(vec_rows[:], 0.0)
        nc.vector.memset(planes[:].bitcast(I32), 0)

        nc.scalar.dma_start(
            out=vec_rows[0 : POSITIONS * CHUNKS, :],
            in_=b1.rearrange("l (c n) -> (l c) n", n=P),
        )
        for v, vector in enumerate((gamma1, beta1, mean1, var1)):
            row = (POSITIONS + v) * CHUNKS
            nc.scalar.dma_start(
                out=vec_rows[row : row + CHUNKS, :],
                in_=vector.rearrange("(c n) -> c n", n=P),
            )

        nc.sync.dma_start(out=x_sb[:], in_=x.rearrange("b l c -> b (l c)"))

        scale_rows = k1_scales.rearrange(
            "(s j) (q r) n -> q r j s n", j=PLANES_PER_SLOT, r=4
        )
        def load_scale_rows(queue, view, quadrant, r):
            first = 32 * quadrant + r
            queue.dma_start(
                out=planes[first : first + 16 : 4, :].bitcast(view),
                in_=scale_rows[quadrant, r].bitcast(view),
            )

        for r in range(4):
            for quadrant in (2, 3):
                load_scale_rows(nc.gpsimd, F32, quadrant, r)
        on_sync = [(quadrant, r) for r in range(4) for quadrant in (0, 1)]

        words_by_position = k1_words.rearrange("(i l) p n t -> l p i (n t)", l=POSITIONS)
        for position in range(POSITIONS):
            for tile, (first, last, left, right) in zip(weights[position], weight_loads(position)):
                nc.sync.dma_start(
                    out=tile[:],
                    in_=words_by_position[
                        position, :, first : last + 1, 4 * left : 4 * (right + 1)
                    ].bitcast(I32),
                )
                for quadrant, r in on_sync[:2]:
                    load_scale_rows(nc.sync, I32, quadrant, r)
                on_sync = on_sync[2:]

        nc.vector.tensor_copy(out=ident_bf16[:], in_=ident_f32[:])

        rows_t = setup_psum.tile([P, P], BF16, tag="setup", name="rows_t")
        nc.tensor.transpose(rows_t[:], vec_rows[:], ident_bf16[:])
        N_COLS = (POSITIONS + 4) * CHUNKS
        cols = keep.tile([P, N_COLS], F32)
        nc.vector.tensor_copy(out=cols[:], in_=rows_t[:, 0:N_COLS])
        b1_c = cols[:, 0 : POSITIONS * CHUNKS].rearrange("p (l c) -> p l c", c=CHUNKS)

        def vec_col(v):
            return cols[:, (POSITIONS + v) * CHUNKS : (POSITIONS + v + 1) * CHUNKS]

        def over_positions(ap):
            return ap.unsqueeze(1).to_broadcast([P, POSITIONS, CHUNKS])

        gamma_c, beta_c, mean_c, var_c = vec_col(0), vec_col(1), vec_col(2), vec_col(3)
        folded = keep.tile([P, (1 + POSITIONS) * CHUNKS], F32)
        gain_c = folded[:, 0:CHUNKS]
        shift_c = folded[:, CHUNKS : (1 + POSITIONS) * CHUNKS].rearrange("p (l c) -> p l c", c=CHUNKS)
        std_c = keep.tile([P, CHUNKS], F32)
        nc.vector.tensor_scalar_add(out=std_c[:], in0=var_c, scalar1=BN_EPS)
        nc.scalar.sqrt(out=std_c[:], in_=std_c[:])
        nc.vector.reciprocal(out=std_c[:], in_=std_c[:])
        nc.vector.tensor_tensor(out=gain_c, in0=gamma_c, in1=std_c[:], op=ALU.mult)
        nc.vector.scalar_tensor_tensor(
            out=shift_c, in0=b1_c, scalar=2.0, in1=over_positions(mean_c),
            op0=ALU.mult, op1=ALU.subtract,
        )
        nc.vector.tensor_tensor(out=shift_c, in0=shift_c, in1=over_positions(gain_c), op=ALU.mult)
        nc.vector.tensor_tensor(out=shift_c, in0=shift_c, in1=over_positions(beta_c), op=ALU.add)

        x_words = x_sb[:].bitcast(F32)
        grouped_words = grouped[:].bitcast(F32)
        WORDS = CHANNELS // 2
        for pair in range(POSITIONS // 2):
            xt = setup_psum.tile([P, 2, 2, P], F32, tag="setup", name="xt")
            for a in range(2):
                first = WORDS * (2 * pair + a)
                for u in range(2):
                    nc.tensor.transpose(
                        xt[:, a, u, :], x_words[:, first + u : first + WORDS : 2], ident_f32[:]
                    )
            dest = grouped_words[:, 2 * WORDS * pair : 2 * WORDS * (pair + 1)].rearrange(
                "p (a b u) -> p a b u", a=2, u=2
            )
            source = xt[:].rearrange("p a u b -> p a b u")
            if pair % 2 == 0:
                nc.vector.tensor_copy(out=dest, in_=source)
            else:
                nc.scalar.copy(out=dest, in_=source)
        for pair in range(POSITIONS // 2):
            nc.vector.quantize_mx(
                out=x_codes[:, 2 * P * pair : 2 * P * (pair + 1)].bitcast(FP8X4),
                scales=x_scales[:, 2 * P * pair : 2 * P * (pair + 1)],
                in_=grouped[:, 2 * CHANNELS * pair : 2 * CHANNELS * (pair + 1)],
            )

        spread = keep.tile([P, 1 + POSITIONS, FILTERS], F32)
        for v in range(1 + POSITIONS):
            spread_ps = setup_psum.tile([P, FILTERS], F32, tag="setup", name="spread_ps")
            for c in range(CHUNKS):
                col = CHUNKS * v + c
                nc.tensor.transpose(
                    spread_ps[:, P * c : P * (c + 1)],
                    folded[:, col : col + 1].to_broadcast([P, P]),
                    ident_f32[:],
                )
            if v % 2 == 0:
                nc.scalar.copy(out=spread[:, v, :], in_=spread_ps[:])
            else:
                nc.vector.tensor_copy(out=spread[:, v, :], in_=spread_ps[:])

        out_rows = out.rearrange("b l f -> b (l f)")
        for position in range(POSITIONS):
            parts = parts_of(position)
            accs = []
            for part, width in parts:
                acc = acc_psum.tile([P, width], F32, tag="acc", name="acc")
                accs.append(acc)
            for tile, (first, last, left, right) in zip(weights[position], weight_loads(position)):
                for tap in range(first, last + 1):
                    x_pos = (position - STEP[tap]) % POSITIONS
                    slot, offset = plane_place(tap, position)
                    for acc, (part, width) in zip(accs, parts):
                        if part < left or part > right:
                            continue
                        column = FILTERS * slot + part
                        nc.tensor.matmul_mx(
                            out=acc[:],
                            lhsT=x_codes[:, P * x_pos : P * (x_pos + 1)].bitcast(FP8X4),
                            lhsT_scale=x_scales[:, P * x_pos : P * (x_pos + 1)],
                            rhs=tile[:, tap - first, part - left : part - left + width].bitcast(FP8X4),
                            rhs_scale=planes[offset:P, column : column + width],
                            start=(tap == 0),
                            stop=(tap == TAPS - 1),
                        )
            for acc, (part, width) in zip(accs, parts):
                z = z_all[:, FILTERS * position + part : FILTERS * position + part + width]
                half = width // 2
                halves = [(slice(h, h + half), slice(part + h, part + h + half)) for h in (0, half)]
                for here, cols in halves:
                    nc.vector.tensor_tensor(
                        out=z[:, here], in0=acc[:, here], in1=spread[:, 0, cols], op=ALU.mult
                    )
                for here, cols in halves:
                    nc.vector.tensor_tensor(
                        out=z[:, here], in0=z[:, here], in1=spread[:, 1 + position, cols], op=ALU.add
                    )
                for here, cols in halves:
                    nc.vector.scalar_tensor_tensor(
                        out=z[:, here], in0=z[:, here], scalar=LEAKY_ALPHA, in1=z[:, here],
                        op0=ALU.mult, op1=ALU.max,
                    )
                if len(parts) > 1:
                    nc.sync.dma_start(out=out[:, position, part : part + width], in_=z)
            for first, last in STORES:
                if last == position:
                    nc.sync.dma_start(
                        out=out_rows[:, FILTERS * first : FILTERS * (last + 1)],
                        in_=z_all[:, FILTERS * first : FILTERS * (last + 1)],
                    )
